import numpy as np
import ml_dtypes


def mxq(x, axis, fmt="e4m3"):
    dtype, down = {"e4m3": (ml_dtypes.float8_e4m3fn, 7), "e5m2": (ml_dtypes.float8_e5m2, 14)}[fmt]
    v = np.moveaxis(np.asarray(x, np.float32).astype(ml_dtypes.bfloat16).astype(np.float64), axis, -1)
    blocks = v.reshape(v.shape[:-1] + (-1, 32))
    amax = np.abs(blocks).max(-1, keepdims=True)
    byte = np.maximum(np.where(amax > 0, np.frexp(amax)[1] - 1 + 127, 0) - down, 1)
    scale = np.exp2(byte - 127.0)
    codes = (blocks / scale).astype(np.float32).astype(dtype).astype(np.float64)
    return np.moveaxis((codes * scale).reshape(v.shape), -1, axis)


WIDE = False


def mx_kscale(k):
    if not WIDE:
        return np.ones(k)
    levels = np.array([20, -20, 10, -10, 0])
    a = np.random.permutation(np.resize(levels, k // 512 * 4)).reshape(k // 512, 4)
    idx = np.arange(k)
    return np.exp2(a[idx // 512, idx % 128 // 32])


BF16 = ml_dtypes.bfloat16


def bf(x):
    return np.asarray(x, np.float32).astype(BF16)


def f64(x):
    return np.asarray(x).astype(np.float64)


B, C, H, W, O = 2, 256, 128, 64, 512
K = 4 * C


def setup_inputs():
    u = mx_kscale(O)
    x = np.random.standard_normal((B, C, H, W))
    w = np.random.standard_normal((O, K, 1, 1)) / np.sqrt(K) / u[:, None, None, None]
    e = np.random.randint(-12, 1, (B, 1, H // 2, W // 2))
    g = np.random.standard_normal((B, O, H // 2, W // 2)) * np.exp2(e) * 8.0 * u[None, :, None, None]
    return {"x": bf(x), "w_fusion": bf(w), "grad_out": bf(g)}


def reference(x, w_fusion, grad_out):
    g = f64(grad_out)
    w = f64(w_fusion)[:, :, 0, 0]
    nb, no, nh, nw = g.shape
    nk = w.shape[1]
    gcomb = np.einsum('bohw,oc->bchw', mxq(g, 1, "e5m2"), mxq(w, 0, "e4m3"), optimize=True)
    gcomb = gcomb.reshape(nb, nk // 4, 4, nh, nw)
    gLL = gcomb[:, :, 0]
    gLH = gcomb[:, :, 1]
    gHL = gcomb[:, :, 2]
    gHH = gcomb[:, :, 3]
    gx = np.zeros((nb, nk // 4, nh, 2, nw, 2))
    gx[:, :, :, 0, :, 0] = (gLL + gLH + gHL + gHH) * 0.5
    gx[:, :, :, 0, :, 1] = (gLL + gLH - gHL - gHH) * 0.5
    gx[:, :, :, 1, :, 0] = (gLL - gLH + gHL - gHH) * 0.5
    gx[:, :, :, 1, :, 1] = (gLL - gLH - gHL + gHH) * 0.5
    return gx.reshape(nb, nk // 4, nh * 2, nw * 2)

@@ -1,0 +1,181 @@
+from contextlib import ExitStack
+
+import concourse.mybir as mybir
+
+F32 = mybir.dt.float32
+BF16 = mybir.dt.bfloat16
+U32 = mybir.dt.uint32
+U8 = mybir.dt.uint8
+E4M3X4 = mybir.dt.float8_e4m3fn_x4
+E5M2X4 = mybir.dt.float8_e5m2_x4
+ALU = mybir.AluOpType
+ACT = mybir.ActivationFunctionType
+
+P = 128
+PACK = 4
+IMAGES = 2
+CHANNELS = 256
+OUT_CH = 512
+BANDS = 4
+BLOCK_ROWS = 64
+BLOCK_COLS = 32
+TOKENS = BLOCK_ROWS * BLOCK_COLS
+N_TILE = 512
+ROWS_TILE = N_TILE // BLOCK_COLS
+TILES_PER_IMAGE = TOKENS // N_TILE
+N_TILES = IMAGES * TILES_PER_IMAGE
+C_BLOCKS = CHANNELS // P
+
+FLOPS = 2 * IMAGES * TOKENS * OUT_CH * CHANNELS * BANDS
+BYTES = 2 * OUT_CH * CHANNELS * BANDS + 2 * IMAGES * OUT_CH * TOKENS + 4 * IMAGES * CHANNELS * TOKENS * 4
+
+LL, LH, HL, HH, NEG_LH, NEG_HH = 0, 1, 2, 3, 4, 5
+
+T1_ON_GPSIMD = False
+VECTOR_REGROUPS = (3, 6)
+MANUAL = False
+AHEAD = 2
+CHUNKS = ((0, 0, 512), (0, 512, 512), (0, 1024, 1024), (1, 0, 2048))
+
+
+def tile_haarwaveletlayer_t_kernel(tc, x, w_fusion, grad_out, out):
+    nc = tc.nc
+    with ExitStack() as ctx:
+        if MANUAL:
+            ctx.enter_context(tc.manual_schedule())
+        keep = ctx.enter_context(tc.tile_pool(name="keep", bufs=1))
+        grp_pool = ctx.enter_context(tc.tile_pool(name="grp", bufs=3))
+        t_pool = ctx.enter_context(tc.tile_pool(name="tplanes", bufs=4))
+        o_pool = ctx.enter_context(tc.tile_pool(name="outs", bufs=6))
+        psum = ctx.enter_context(tc.psum_pool(name="psum", bufs=4))
+
+        w_view = w_fusion.rearrange("(p j) k a b -> p j (k a b)", j=PACK)
+        half_k = P * BANDS
+
+        w_raw = []
+        g_raw = []
+
+        def load_w(cb):
+            raw = keep.tile([P, PACK, half_k], BF16, name="w_raw%d" % cb)
+            nc.sync.dma_start(out=raw[:], in_=w_view[:, :, cb * half_k : (cb + 1) * half_k])
+            w_raw.append(raw)
+
+        def load_g(i):
+            b, t0, n = CHUNKS[i]
+            raw = keep.tile([P, PACK, n], BF16, name="g_raw%d" % i)
+            g_view = grad_out[b].rearrange("(p j) h w -> p j (h w)", j=PACK)
+            nc.sync.dma_start(out=raw[:], in_=g_view[:, :, t0 : t0 + n])
+            g_raw.append(raw)
+
+        load_w(0)
+        load_g(0)
+        load_w(1)
+        for i in range(1, len(CHUNKS)):
+            load_g(i)
+
+        w_codes = []
+        w_scales = []
+
+        def prep_w(cb):
+            grp = keep.tile([P, 6, P, PACK], BF16, name="w_grp%d" % cb, align_bytes=64)
+            nc.vector.tensor_copy(
+                out=grp[:, 0:4, :, :],
+                in_=w_raw[cb][:].rearrange("p j (c v) -> p v c j", v=BANDS),
+            )
+            nc.vector.tensor_scalar_mul(out=grp[:, 4:6, :, :], in0=grp[:, 1:4:2, :, :], scalar1=-1.0)
+            codes = keep.tile([P, 6 * P], U32, name="w_codes%d" % cb, align_bytes=64)
+            scales = keep.tile([P, 6 * P], U8, name="w_scales%d" % cb, align_bytes=64)
+            nc.vector.quantize_mx(
+                out=codes[:, 0 : 4 * P].bitcast(E4M3X4),
+                scales=scales[:, 0 : 4 * P],
+                in_=grp[:, 0:4, :, :].rearrange("p v c j -> p (v c j)"),
+            )
+            nc.vector.quantize_mx(
+                out=codes[:, 4 * P : 6 * P].bitcast(E4M3X4),
+                scales=scales[:, 4 * P : 6 * P],
+                in_=grp[:, 4:6, :, :].rearrange("p v c j -> p (v c j)"),
+            )
+            w_codes.append(codes)
+            w_scales.append(scales)
+
+        g_codes = {}
+        g_scales = {}
+
+        def prep_g(tt):
+            b = tt // TILES_PER_IMAGE
+            t0 = (tt % TILES_PER_IMAGE) * N_TILE
+            src = None
+            for i, (cb_, c0, n) in enumerate(CHUNKS):
+                if cb_ == b and c0 <= t0 and t0 + N_TILE <= c0 + n:
+                    src = g_raw[i][:, :, t0 - c0 : t0 - c0 + N_TILE]
+            grp = grp_pool.tile([P, N_TILE, PACK], BF16, name="g_grp", align_bytes=64)
+            dst_v = grp[:].rearrange("p (c i) t -> p c t i", i=4)
+            src_v = src.rearrange("p t (c i) -> p c t i", i=4)
+            if tt in VECTOR_REGROUPS:
+                nc.vector.tensor_copy(out=dst_v, in_=src_v)
+            else:
+                nc.scalar.copy(out=dst_v, in_=src_v)
+            codes = keep.tile([P, N_TILE], U32, name="g_codes%d" % tt, align_bytes=64)
+            scales = keep.tile([P, N_TILE], U8, name="g_scales%d" % tt, align_bytes=64)
+            nc.vector.quantize_mx(
+                out=codes[:].bitcast(E5M2X4),
+                scales=scales[:],
+                in_=grp[:].rearrange("p n t -> p (n t)"),
+            )
+            g_codes[tt] = codes
+            g_scales[tt] = scales
+
+        def mx_pair(acc, tt, cb, first, second):
+            for k, v in enumerate((first, second)):
+                nc.tensor.matmul_mx(
+                    out=acc[:],
+                    lhsT=w_codes[cb][:, v * P : (v + 1) * P].bitcast(E4M3X4),
+                    lhsT_scale=w_scales[cb][:, v * P : (v + 1) * P],
+                    rhs=g_codes[tt][:].bitcast(E5M2X4),
+                    rhs_scale=g_scales[tt][:],
+                    start=(k == 0),
+                    stop=(k == 1),
+                )
+
+        def compute(tt, cb):
+            b = tt // TILES_PER_IMAGE
+            y0 = (tt % TILES_PER_IMAGE) * ROWS_TILE * 2
+            o_tile = o_pool.tile([P, ROWS_TILE, 2, 2 * BLOCK_COLS], F32, name="o_tile")
+            for di in range(2):
+                t_ps = psum.tile([P, N_TILE], F32, name="t_ps")
+                mx_pair(t_ps, tt, cb, HL, HH if di == 0 else NEG_HH)
+                s_ps = psum.tile([P, N_TILE], F32, name="s_ps")
+                mx_pair(s_ps, tt, cb, LL, LH if di == 0 else NEG_LH)
+                planes = t_pool.tile([P, 2, N_TILE], F32, name="planes")
+                nc.scalar.activation(out=planes[:, 0, :], in_=t_ps[:], func=ACT.Copy, scale=0.5)
+                if T1_ON_GPSIMD:
+                    nc.gpsimd.tensor_scalar(
+                        out=planes[:, 1, :], in0=planes[:, 0, :], scalar1=-1.0, scalar2=0.0,
+                        op0=ALU.mult, op1=ALU.add,
+                    )
+                else:
+                    nc.scalar.activation(out=planes[:, 1, :], in_=t_ps[:], func=ACT.Copy, scale=-0.5)
+                shape = [P, ROWS_TILE, BLOCK_COLS, 2]
+                nc.vector.scalar_tensor_tensor(
+                    out=o_tile[:, :, di, :].rearrange("p i (j d) -> p i j d", d=2),
+                    in0=s_ps[:].rearrange("p (i j) -> p i j", j=BLOCK_COLS).unsqueeze(3).to_broadcast(shape),
+                    scalar=0.5,
+                    in1=planes[:].rearrange("p d (i j) -> p i j d", j=BLOCK_COLS),
+                    op0=ALU.mult,
+                    op1=ALU.add,
+                )
+            nc.sync.dma_start(
+                out=out[b, cb * P : (cb + 1) * P, y0 : y0 + 2 * ROWS_TILE, :].rearrange("c y x -> c (y x)"),
+                in_=o_tile[:].rearrange("p i d x -> p (i d x)"),
+            )
+
+        prep_w(0)
+        prep_g(0)
+        prep_w(1)
+        for tt in range(1, AHEAD):
+            prep_g(tt)
+        for tt in range(N_TILES):
+            if tt + AHEAD < N_TILES:
+                prep_g(tt + AHEAD)
+            for cb in range(C_BLOCKS):
+                compute(tt, cb)

@@ -31,8 +31,8 @@ BYTES = 2 * OUT_CH * CHANNELS * BANDS + 2 * IMAGES * OUT_CH * TOKENS + 4 * IMAGE
 
 LL, LH, HL, HH, NEG_LH, NEG_HH = 0, 1, 2, 3, 4, 5
 
-T1_ON_GPSIMD = False
-VECTOR_REGROUPS = (3, 6)
+T1_ON_GPSIMD = True
+VECTOR_REGROUPS = ()
 MANUAL = False
 AHEAD = 2
 CHUNKS = ((0, 0, 512), (0, 512, 512), (0, 1024, 1024), (1, 0, 2048))
@@ -45,7 +45,7 @@ def tile_haarwaveletlayer_t_kernel(tc, x, w_fusion, grad_out, out):
             ctx.enter_context(tc.manual_schedule())
         keep = ctx.enter_context(tc.tile_pool(name="keep", bufs=1))
         grp_pool = ctx.enter_context(tc.tile_pool(name="grp", bufs=3))
-        t_pool = ctx.enter_context(tc.tile_pool(name="tplanes", bufs=4))
+        t_pool = ctx.enter_context(tc.tile_pool(name="tplanes", bufs=6))
         o_pool = ctx.enter_context(tc.tile_pool(name="outs", bufs=6))
         psum = ctx.enter_context(tc.psum_pool(name="psum", bufs=4))
 

@@ -31,11 +31,12 @@ BYTES = 2 * OUT_CH * CHANNELS * BANDS + 2 * IMAGES * OUT_CH * TOKENS + 4 * IMAGE
 
 LL, LH, HL, HH, NEG_LH, NEG_HH = 0, 1, 2, 3, 4, 5
 
-T1_ON_GPSIMD = True
-VECTOR_REGROUPS = ()
-MANUAL = False
-AHEAD = 2
+MANUAL = True
 CHUNKS = ((0, 0, 512), (0, 512, 512), (0, 1024, 1024), (1, 0, 2048))
+PIECES = 4
+EARLY_PIECES = 3
+T_BANKS = 3
+S_BANKS = 5
 
 
 def tile_haarwaveletlayer_t_kernel(tc, x, w_fusion, grad_out, out):
@@ -47,80 +48,87 @@ def tile_haarwaveletlayer_t_kernel(tc, x, w_fusion, grad_out, out):
         grp_pool = ctx.enter_context(tc.tile_pool(name="grp", bufs=3))
         t_pool = ctx.enter_context(tc.tile_pool(name="tplanes", bufs=6))
         o_pool = ctx.enter_context(tc.tile_pool(name="outs", bufs=6))
-        psum = ctx.enter_context(tc.psum_pool(name="psum", bufs=4))
+        psum_t = ctx.enter_context(tc.psum_pool(name="psum_t", bufs=T_BANKS))
+        psum_s = ctx.enter_context(tc.psum_pool(name="psum_s", bufs=S_BANKS))
 
         w_view = w_fusion.rearrange("(p j) k a b -> p j (k a b)", j=PACK)
         half_k = P * BANDS
 
-        w_raw = []
-        g_raw = []
+        w_raw = {}
+        g_raw = {}
 
         def load_w(cb):
             raw = keep.tile([P, PACK, half_k], BF16, name="w_raw%d" % cb)
             nc.sync.dma_start(out=raw[:], in_=w_view[:, :, cb * half_k : (cb + 1) * half_k])
-            w_raw.append(raw)
+            w_raw[cb] = raw
 
         def load_g(i):
             b, t0, n = CHUNKS[i]
             raw = keep.tile([P, PACK, n], BF16, name="g_raw%d" % i)
             g_view = grad_out[b].rearrange("(p j) h w -> p j (h w)", j=PACK)
             nc.sync.dma_start(out=raw[:], in_=g_view[:, :, t0 : t0 + n])
-            g_raw.append(raw)
+            g_raw[i] = raw
 
-        load_w(0)
         load_g(0)
+        load_w(0)
         load_w(1)
         for i in range(1, len(CHUNKS)):
             load_g(i)
 
-        w_codes = []
-        w_scales = []
+        w_grp = {}
+        w_codes = {}
+        w_scales = {}
 
-        def prep_w(cb):
-            grp = keep.tile([P, 6, P, PACK], BF16, name="w_grp%d" % cb, align_bytes=64)
+        def w_tiles(cb):
+            w_grp[cb] = keep.tile([P, 6, P, PACK], BF16, name="w_grp%d" % cb, align_bytes=64)
+            w_codes[cb] = keep.tile([P, 6 * P], U32, name="w_codes%d" % cb, align_bytes=64)
+            w_scales[cb] = keep.tile([P, 6 * P], U8, name="w_scales%d" % cb, align_bytes=64)
+
+        def w_regroup(cb, v0, v1):
             nc.vector.tensor_copy(
-                out=grp[:, 0:4, :, :],
-                in_=w_raw[cb][:].rearrange("p j (c v) -> p v c j", v=BANDS),
+                out=w_grp[cb][:, v0:v1, :, :],
+                in_=w_raw[cb][:].rearrange("p j (c v) -> p v c j", v=BANDS)[:, v0:v1, :, :],
             )
-            nc.vector.tensor_scalar_mul(out=grp[:, 4:6, :, :], in0=grp[:, 1:4:2, :, :], scalar1=-1.0)
-            codes = keep.tile([P, 6 * P], U32, name="w_codes%d" % cb, align_bytes=64)
-            scales = keep.tile([P, 6 * P], U8, name="w_scales%d" % cb, align_bytes=64)
-            nc.vector.quantize_mx(
-                out=codes[:, 0 : 4 * P].bitcast(E4M3X4),
-                scales=scales[:, 0 : 4 * P],
-                in_=grp[:, 0:4, :, :].rearrange("p v c j -> p (v c j)"),
-            )
-            nc.vector.quantize_mx(
-                out=codes[:, 4 * P : 6 * P].bitcast(E4M3X4),
-                scales=scales[:, 4 * P : 6 * P],
-                in_=grp[:, 4:6, :, :].rearrange("p v c j -> p (v c j)"),
-            )
-            w_codes.append(codes)
-            w_scales.append(scales)
 
+        def w_negate(cb):
+            nc.vector.tensor_scalar_mul(
+                out=w_grp[cb][:, 4:6, :, :], in0=w_grp[cb][:, 1:4:2, :, :], scalar1=-1.0
+            )
+
+        def w_quantise(cb, v0, v1):
+            nc.vector.quantize_mx(
+                out=w_codes[cb][:, v0 * P : v1 * P].bitcast(E4M3X4),
+                scales=w_scales[cb][:, v0 * P : v1 * P],
+                in_=w_grp[cb][:, v0:v1, :, :].rearrange("p v c j -> p (v c j)"),
+            )
+
+        g_grp = {}
         g_codes = {}
         g_scales = {}
 
-        def prep_g(tt):
+        def g_piece(tt, n0, n1, on_vector):
             b = tt // TILES_PER_IMAGE
             t0 = (tt % TILES_PER_IMAGE) * N_TILE
             src = None
             for i, (cb_, c0, n) in enumerate(CHUNKS):
                 if cb_ == b and c0 <= t0 and t0 + N_TILE <= c0 + n:
                     src = g_raw[i][:, :, t0 - c0 : t0 - c0 + N_TILE]
-            grp = grp_pool.tile([P, N_TILE, PACK], BF16, name="g_grp", align_bytes=64)
-            dst_v = grp[:].rearrange("p (c i) t -> p c t i", i=4)
-            src_v = src.rearrange("p t (c i) -> p c t i", i=4)
-            if tt in VECTOR_REGROUPS:
+            if tt not in g_grp:
+                g_grp[tt] = grp_pool.tile([P, N_TILE, PACK], BF16, name="g_grp", align_bytes=64)
+            dst_v = g_grp[tt][:, n0:n1, :].rearrange("p (c i) t -> p c t i", i=4)
+            src_v = src[:, :, n0:n1].rearrange("p t (c i) -> p c t i", i=4)
+            if on_vector:
                 nc.vector.tensor_copy(out=dst_v, in_=src_v)
             else:
                 nc.scalar.copy(out=dst_v, in_=src_v)
+
+        def g_quantise(tt):
             codes = keep.tile([P, N_TILE], U32, name="g_codes%d" % tt, align_bytes=64)
             scales = keep.tile([P, N_TILE], U8, name="g_scales%d" % tt, align_bytes=64)
             nc.vector.quantize_mx(
                 out=codes[:].bitcast(E5M2X4),
                 scales=scales[:],
-                in_=grp[:].rearrange("p n t -> p (n t)"),
+                in_=g_grp[tt][:].rearrange("p n t -> p (n t)"),
             )
             g_codes[tt] = codes
             g_scales[tt] = scales
@@ -137,45 +145,68 @@ def tile_haarwaveletlayer_t_kernel(tc, x, w_fusion, grad_out, out):
                     stop=(k == 1),
                 )
 
-        def compute(tt, cb):
-            b = tt // TILES_PER_IMAGE
-            y0 = (tt % TILES_PER_IMAGE) * ROWS_TILE * 2
-            o_tile = o_pool.tile([P, ROWS_TILE, 2, 2 * BLOCK_COLS], F32, name="o_tile")
-            for di in range(2):
-                t_ps = psum.tile([P, N_TILE], F32, name="t_ps")
-                mx_pair(t_ps, tt, cb, HL, HH if di == 0 else NEG_HH)
-                s_ps = psum.tile([P, N_TILE], F32, name="s_ps")
-                mx_pair(s_ps, tt, cb, LL, LH if di == 0 else NEG_LH)
-                planes = t_pool.tile([P, 2, N_TILE], F32, name="planes")
-                nc.scalar.activation(out=planes[:, 0, :], in_=t_ps[:], func=ACT.Copy, scale=0.5)
-                if T1_ON_GPSIMD:
-                    nc.gpsimd.tensor_scalar(
-                        out=planes[:, 1, :], in0=planes[:, 0, :], scalar1=-1.0, scalar2=0.0,
-                        op0=ALU.mult, op1=ALU.add,
-                    )
-                else:
-                    nc.scalar.activation(out=planes[:, 1, :], in_=t_ps[:], func=ACT.Copy, scale=-0.5)
-                shape = [P, ROWS_TILE, BLOCK_COLS, 2]
-                nc.vector.scalar_tensor_tensor(
-                    out=o_tile[:, :, di, :].rearrange("p i (j d) -> p i j d", d=2),
-                    in0=s_ps[:].rearrange("p (i j) -> p i j", j=BLOCK_COLS).unsqueeze(3).to_broadcast(shape),
-                    scalar=0.5,
-                    in1=planes[:].rearrange("p d (i j) -> p i j d", j=BLOCK_COLS),
-                    op0=ALU.mult,
-                    op1=ALU.add,
-                )
-            nc.sync.dma_start(
-                out=out[b, cb * P : (cb + 1) * P, y0 : y0 + 2 * ROWS_TILE, :].rearrange("c y x -> c (y x)"),
-                in_=o_tile[:].rearrange("p i d x -> p (i d x)"),
-            )
+        w_tiles(0)
+        w_tiles(1)
+        g_piece(0, 0, N_TILE // 2, False)
+        g_piece(0, N_TILE // 2, N_TILE, True)
+        w_regroup(0, 2, 4)
+        g_quantise(0)
+        w_regroup(0, 0, 2)
+        w_quantise(0, 2, 4)
+        w_negate(0)
+        w_quantise(0, 0, 2)
+        w_quantise(0, 4, 6)
+        w_regroup(1, 0, 4)
+        w_negate(1)
+        w_quantise(1, 0, 4)
+        w_quantise(1, 4, 6)
 
-        prep_w(0)
-        prep_g(0)
-        prep_w(1)
-        for tt in range(1, AHEAD):
-            prep_g(tt)
-        for tt in range(N_TILES):
-            if tt + AHEAD < N_TILES:
-                prep_g(tt + AHEAD)
-            for cb in range(C_BLOCKS):
-                compute(tt, cb)
+        step = N_TILE // PIECES
+        pieces = [(tt, q) for tt in range(1, N_TILES) for q in range(PIECES)]
+        done = {}
+
+        def next_piece():
+            if pieces:
+                tt, q = pieces.pop(0)
+                g_piece(tt, q * step, (q + 1) * step, False)
+                done[tt] = q + 1
+
+        for k in range(EARLY_PIECES):
+            next_piece()
+
+        next_q = 1
+        o_tile = None
+        shape = [P, ROWS_TILE, BLOCK_COLS, 2]
+        for h in range(4 * N_TILES):
+            tt, cb, di = h // 4, (h // 2) % 2, h % 2
+            t_ps = psum_t.tile([P, N_TILE], F32, name="t_ps")
+            mx_pair(t_ps, tt, cb, HL, HH if di == 0 else NEG_HH)
+            s_ps = psum_s.tile([P, N_TILE], F32, name="s_ps")
+            mx_pair(s_ps, tt, cb, LL, LH if di == 0 else NEG_LH)
+            planes = t_pool.tile([P, 2, N_TILE], F32, name="planes")
+            nc.scalar.activation(out=planes[:, 0, :], in_=t_ps[:], func=ACT.Copy, scale=0.5)
+            next_piece()
+            nc.gpsimd.tensor_scalar(
+                out=planes[:, 1, :], in0=planes[:, 0, :], scalar1=-1.0, scalar2=0.0,
+                op0=ALU.mult, op1=ALU.add,
+            )
+            if di == 0:
+                o_tile = o_pool.tile([P, ROWS_TILE, 2, 2 * BLOCK_COLS], F32, name="o_tile")
+            nc.vector.scalar_tensor_tensor(
+                out=o_tile[:, :, di, :].rearrange("p i (j d) -> p i j d", d=2),
+                in0=s_ps[:].rearrange("p (i j) -> p i j", j=BLOCK_COLS).unsqueeze(3).to_broadcast(shape),
+                scalar=0.5,
+                in1=planes[:].rearrange("p d (i j) -> p i j d", j=BLOCK_COLS),
+                op0=ALU.mult,
+                op1=ALU.add,
+            )
+            if next_q < N_TILES and done.get(next_q, 0) == PIECES:
+                g_quantise(next_q)
+                next_q += 1
+            if di == 1:
+                b = tt // TILES_PER_IMAGE
+                y0 = (tt % TILES_PER_IMAGE) * ROWS_TILE * 2
+                nc.sync.dma_start(
+                    out=out[b, cb * P : (cb + 1) * P, y0 : y0 + 2 * ROWS_TILE, :].rearrange("c y x -> c (y x)"),
+                    in_=o_tile[:].rearrange("p i d x -> p (i d x)"),
+                )

@@ -35,6 +35,8 @@ MANUAL = True
 CHUNKS = ((0, 0, 512), (0, 512, 512), (0, 1024, 1024), (1, 0, 2048))
 PIECES = 4
 EARLY_PIECES = 3
+TAIL_SPLIT = 2
+TAIL_UNITS = 2
 T_BANKS = 3
 S_BANKS = 5
 
@@ -69,8 +71,8 @@ def tile_haarwaveletlayer_t_kernel(tc, x, w_fusion, grad_out, out):
             nc.sync.dma_start(out=raw[:], in_=g_view[:, :, t0 : t0 + n])
             g_raw[i] = raw
 
-        load_g(0)
         load_w(0)
+        load_g(0)
         load_w(1)
         for i in range(1, len(CHUNKS)):
             load_g(i)
@@ -145,15 +147,27 @@ def tile_haarwaveletlayer_t_kernel(tc, x, w_fusion, grad_out, out):
                     stop=(k == 1),
                 )
 
+        def butterfly(o_tile, di, s_ps, planes, r0, rows):
+            n0 = r0 * BLOCK_COLS
+            n1 = (r0 + rows) * BLOCK_COLS
+            nc.vector.scalar_tensor_tensor(
+                out=o_tile[:, :, di, :].rearrange("p i (j d) -> p i j d", d=2),
+                in0=s_ps[:, n0:n1].rearrange("p (i j) -> p i j", j=BLOCK_COLS).unsqueeze(3).to_broadcast([P, rows, BLOCK_COLS, 2]),
+                scalar=0.5,
+                in1=planes[:, :, n0:n1].rearrange("p d (i j) -> p i j d", j=BLOCK_COLS),
+                op0=ALU.mult,
+                op1=ALU.add,
+            )
+
         w_tiles(0)
         w_tiles(1)
         g_piece(0, 0, N_TILE // 2, False)
-        g_piece(0, N_TILE // 2, N_TILE, True)
         w_regroup(0, 2, 4)
-        g_quantise(0)
         w_regroup(0, 0, 2)
+        g_piece(0, N_TILE // 2, N_TILE, True)
         w_quantise(0, 2, 4)
         w_negate(0)
+        g_quantise(0)
         w_quantise(0, 0, 2)
         w_quantise(0, 4, 6)
         w_regroup(1, 0, 4)
@@ -175,10 +189,11 @@ def tile_haarwaveletlayer_t_kernel(tc, x, w_fusion, grad_out, out):
             next_piece()
 
         next_q = 1
-        o_tile = None
-        shape = [P, ROWS_TILE, BLOCK_COLS, 2]
+        halves = []
         for h in range(4 * N_TILES):
             tt, cb, di = h // 4, (h // 2) % 2, h % 2
+            splits = TAIL_SPLIT if h // 2 >= 2 * N_TILES - TAIL_UNITS else 1
+            rows = ROWS_TILE // splits
             t_ps = psum_t.tile([P, N_TILE], F32, name="t_ps")
             mx_pair(t_ps, tt, cb, HL, HH if di == 0 else NEG_HH)
             s_ps = psum_s.tile([P, N_TILE], F32, name="s_ps")
@@ -191,22 +206,25 @@ def tile_haarwaveletlayer_t_kernel(tc, x, w_fusion, grad_out, out):
                 op0=ALU.mult, op1=ALU.add,
             )
             if di == 0:
-                o_tile = o_pool.tile([P, ROWS_TILE, 2, 2 * BLOCK_COLS], F32, name="o_tile")
-            nc.vector.scalar_tensor_tensor(
-                out=o_tile[:, :, di, :].rearrange("p i (j d) -> p i j d", d=2),
-                in0=s_ps[:].rearrange("p (i j) -> p i j", j=BLOCK_COLS).unsqueeze(3).to_broadcast(shape),
-                scalar=0.5,
-                in1=planes[:].rearrange("p d (i j) -> p i j d", j=BLOCK_COLS),
-                op0=ALU.mult,
-                op1=ALU.add,
-            )
+                halves = []
+            halves.append((s_ps, planes))
+            b = tt // TILES_PER_IMAGE
+            y0 = (tt % TILES_PER_IMAGE) * ROWS_TILE * 2
+            if splits == 1:
+                if di == 0:
+                    o_tile = o_pool.tile([P, rows, 2, 2 * BLOCK_COLS], F32, name="o_tile")
+                butterfly(o_tile, di, s_ps, planes, 0, rows)
             if next_q < N_TILES and done.get(next_q, 0) == PIECES:
                 g_quantise(next_q)
                 next_q += 1
             if di == 1:
-                b = tt // TILES_PER_IMAGE
-                y0 = (tt % TILES_PER_IMAGE) * ROWS_TILE * 2
-                nc.sync.dma_start(
-                    out=out[b, cb * P : (cb + 1) * P, y0 : y0 + 2 * ROWS_TILE, :].rearrange("c y x -> c (y x)"),
-                    in_=o_tile[:].rearrange("p i d x -> p (i d x)"),
-                )
+                for r in range(splits):
+                    if splits > 1:
+                        o_tile = o_pool.tile([P, rows, 2, 2 * BLOCK_COLS], F32, name="o_tile")
+                        for dd in range(2):
+                            butterfly(o_tile, dd, halves[dd][0], halves[dd][1], r * rows, rows)
+                    ya = y0 + 2 * rows * r
+                    nc.sync.dma_start(
+                        out=out[b, cb * P : (cb + 1) * P, ya : ya + 2 * rows, :].rearrange("c y x -> c (y x)"),
+                        in_=o_tile[:].rearrange("p i d x -> p (i d x)"),
+                    )

@@ -20,23 +20,24 @@ BANDS = 4
 BLOCK_ROWS = 64
 BLOCK_COLS = 32
 TOKENS = BLOCK_ROWS * BLOCK_COLS
-N_TILE = 512
-ROWS_TILE = N_TILE // BLOCK_COLS
-TILES_PER_IMAGE = TOKENS // N_TILE
+TILE = 512
+TILE_ROWS = TILE // BLOCK_COLS
+TILES_PER_IMAGE = TOKENS // TILE
 N_TILES = IMAGES * TILES_PER_IMAGE
 C_BLOCKS = CHANNELS // P
+HALF_UNITS = N_TILES * C_BLOCKS * 2
 
 FLOPS = 2 * IMAGES * TOKENS * OUT_CH * CHANNELS * BANDS
-BYTES = 2 * OUT_CH * CHANNELS * BANDS + 2 * IMAGES * OUT_CH * TOKENS + 4 * IMAGES * CHANNELS * TOKENS * 4
+BYTES = 2 * OUT_CH * CHANNELS * BANDS + 2 * IMAGES * OUT_CH * TOKENS + 4 * IMAGES * CHANNELS * 4 * TOKENS
 
 LL, LH, HL, HH, NEG_LH, NEG_HH = 0, 1, 2, 3, 4, 5
+N_STATIONARY = 6
 
-MANUAL = True
-CHUNKS = ((0, 0, 512), (0, 512, 512), (0, 1024, 1024), (1, 0, 2048))
-PIECES = 4
-EARLY_PIECES = 3
-TAIL_SPLIT = 2
-TAIL_UNITS = 2
+G_LOADS = ((0, 0, 1), (0, 1, 1), (0, 2, 2), (1, 0, 4))
+
+QUARTER = TILE // 4
+QUARTERS_AHEAD = 3
+
 T_BANKS = 3
 S_BANKS = 5
 
@@ -44,187 +45,163 @@ S_BANKS = 5
 def tile_haarwaveletlayer_t_kernel(tc, x, w_fusion, grad_out, out):
     nc = tc.nc
     with ExitStack() as ctx:
-        if MANUAL:
-            ctx.enter_context(tc.manual_schedule())
+        ctx.enter_context(tc.manual_schedule())
         keep = ctx.enter_context(tc.tile_pool(name="keep", bufs=1))
-        grp_pool = ctx.enter_context(tc.tile_pool(name="grp", bufs=3))
-        t_pool = ctx.enter_context(tc.tile_pool(name="tplanes", bufs=6))
-        o_pool = ctx.enter_context(tc.tile_pool(name="outs", bufs=6))
-        psum_t = ctx.enter_context(tc.psum_pool(name="psum_t", bufs=T_BANKS))
-        psum_s = ctx.enter_context(tc.psum_pool(name="psum_s", bufs=S_BANKS))
+        grouped_pool = ctx.enter_context(tc.tile_pool(name="grouped", bufs=3))
+        plane_pool = ctx.enter_context(tc.tile_pool(name="planes", bufs=6))
+        out_pool = ctx.enter_context(tc.tile_pool(name="outs", bufs=6))
+        t_pool = ctx.enter_context(tc.psum_pool(name="t_banks", bufs=T_BANKS))
+        s_pool = ctx.enter_context(tc.psum_pool(name="s_banks", bufs=S_BANKS))
 
-        w_view = w_fusion.rearrange("(p j) k a b -> p j (k a b)", j=PACK)
-        half_k = P * BANDS
-
+        w_rows = w_fusion.rearrange("(p r) k a b -> p r (k a b)", r=PACK)
+        block_cols = P * BANDS
         w_raw = {}
         g_raw = {}
 
-        def load_w(cb):
-            raw = keep.tile([P, PACK, half_k], BF16, name="w_raw%d" % cb)
-            nc.sync.dma_start(out=raw[:], in_=w_view[:, :, cb * half_k : (cb + 1) * half_k])
-            w_raw[cb] = raw
+        def load_weights(cb):
+            w_raw[cb] = keep.tile([P, PACK, block_cols], BF16, name="w_raw%d" % cb)
+            nc.sync.dma_start(out=w_raw[cb][:], in_=w_rows[:, :, cb * block_cols : (cb + 1) * block_cols])
 
-        def load_g(i):
-            b, t0, n = CHUNKS[i]
-            raw = keep.tile([P, PACK, n], BF16, name="g_raw%d" % i)
-            g_view = grad_out[b].rearrange("(p j) h w -> p j (h w)", j=PACK)
-            nc.sync.dma_start(out=raw[:], in_=g_view[:, :, t0 : t0 + n])
-            g_raw[i] = raw
+        def load_tokens(image, first, tiles):
+            raw = keep.tile([P, PACK, tiles * TILE], BF16, name="g_raw%d_%d" % (image, first))
+            g_rows = grad_out[image].rearrange("(p r) h w -> p r (h w)", r=PACK)
+            nc.sync.dma_start(out=raw[:], in_=g_rows[:, :, first * TILE : (first + tiles) * TILE])
+            for k in range(tiles):
+                g_raw[image * TILES_PER_IMAGE + first + k] = raw[:, :, k * TILE : (k + 1) * TILE]
 
-        load_w(0)
-        load_g(0)
-        load_w(1)
-        for i in range(1, len(CHUNKS)):
-            load_g(i)
+        load_weights(0)
+        load_tokens(*G_LOADS[0])
+        load_weights(1)
+        for g_load in G_LOADS[1:]:
+            load_tokens(*g_load)
 
-        w_grp = {}
-        w_codes = {}
+        w_grouped = {}
+        w_words = {}
         w_scales = {}
+        for cb in range(C_BLOCKS):
+            w_grouped[cb] = keep.tile([P, N_STATIONARY, P, PACK], BF16, name="w_grouped%d" % cb, align_bytes=64)
+            w_words[cb] = keep.tile([P, N_STATIONARY * P], U32, name="w_words%d" % cb, align_bytes=64)
+            w_scales[cb] = keep.tile([P, N_STATIONARY * P], U8, name="w_scales%d" % cb, align_bytes=64)
 
-        def w_tiles(cb):
-            w_grp[cb] = keep.tile([P, 6, P, PACK], BF16, name="w_grp%d" % cb, align_bytes=64)
-            w_codes[cb] = keep.tile([P, 6 * P], U32, name="w_codes%d" % cb, align_bytes=64)
-            w_scales[cb] = keep.tile([P, 6 * P], U8, name="w_scales%d" % cb, align_bytes=64)
-
-        def w_regroup(cb, v0, v1):
+        def regroup_weights(cb, first, last):
             nc.vector.tensor_copy(
-                out=w_grp[cb][:, v0:v1, :, :],
-                in_=w_raw[cb][:].rearrange("p j (c v) -> p v c j", v=BANDS)[:, v0:v1, :, :],
+                out=w_grouped[cb][:, first:last, :, :],
+                in_=w_raw[cb][:].rearrange("p r (c v) -> p v c r", v=BANDS)[:, first:last, :, :],
             )
 
-        def w_negate(cb):
+        def negate_weights(cb):
             nc.vector.tensor_scalar_mul(
-                out=w_grp[cb][:, 4:6, :, :], in0=w_grp[cb][:, 1:4:2, :, :], scalar1=-1.0
+                out=w_grouped[cb][:, NEG_LH : NEG_HH + 1, :, :],
+                in0=w_grouped[cb][:, LH : HH + 1 : 2, :, :],
+                scalar1=-1.0,
             )
 
-        def w_quantise(cb, v0, v1):
+        def quantise_weights(cb, first, last):
             nc.vector.quantize_mx(
-                out=w_codes[cb][:, v0 * P : v1 * P].bitcast(E4M3X4),
-                scales=w_scales[cb][:, v0 * P : v1 * P],
-                in_=w_grp[cb][:, v0:v1, :, :].rearrange("p v c j -> p (v c j)"),
+                out=w_words[cb][:, first * P : last * P].bitcast(E4M3X4),
+                scales=w_scales[cb][:, first * P : last * P],
+                in_=w_grouped[cb][:, first:last, :, :].rearrange("p v c r -> p (v c r)"),
             )
 
-        g_grp = {}
-        g_codes = {}
+        g_grouped = {}
+        g_words = {}
         g_scales = {}
 
-        def g_piece(tt, n0, n1, on_vector):
-            b = tt // TILES_PER_IMAGE
-            t0 = (tt % TILES_PER_IMAGE) * N_TILE
-            src = None
-            for i, (cb_, c0, n) in enumerate(CHUNKS):
-                if cb_ == b and c0 <= t0 and t0 + N_TILE <= c0 + n:
-                    src = g_raw[i][:, :, t0 - c0 : t0 - c0 + N_TILE]
-            if tt not in g_grp:
-                g_grp[tt] = grp_pool.tile([P, N_TILE, PACK], BF16, name="g_grp", align_bytes=64)
-            dst_v = g_grp[tt][:, n0:n1, :].rearrange("p (c i) t -> p c t i", i=4)
-            src_v = src[:, :, n0:n1].rearrange("p t (c i) -> p c t i", i=4)
+        def regroup_tokens(tile, first, last, on_vector):
+            if tile not in g_grouped:
+                g_grouped[tile] = grouped_pool.tile([P, TILE, PACK], BF16, name="g_grouped", align_bytes=64)
+            dst = g_grouped[tile][:, first:last, :].rearrange("p (c i) r -> p c r i", i=4)
+            src = g_raw[tile][:, :, first:last].rearrange("p r (c i) -> p c r i", i=4)
             if on_vector:
-                nc.vector.tensor_copy(out=dst_v, in_=src_v)
+                nc.vector.tensor_copy(out=dst, in_=src)
             else:
-                nc.scalar.copy(out=dst_v, in_=src_v)
+                nc.scalar.copy(out=dst, in_=src)
 
-        def g_quantise(tt):
-            codes = keep.tile([P, N_TILE], U32, name="g_codes%d" % tt, align_bytes=64)
-            scales = keep.tile([P, N_TILE], U8, name="g_scales%d" % tt, align_bytes=64)
+        def quantise_tokens(tile):
+            g_words[tile] = keep.tile([P, TILE], U32, name="g_words%d" % tile, align_bytes=64)
+            g_scales[tile] = keep.tile([P, TILE], U8, name="g_scales%d" % tile, align_bytes=64)
             nc.vector.quantize_mx(
-                out=codes[:].bitcast(E5M2X4),
-                scales=scales[:],
-                in_=g_grp[tt][:].rearrange("p n t -> p (n t)"),
+                out=g_words[tile][:].bitcast(E5M2X4),
+                scales=g_scales[tile][:],
+                in_=g_grouped[tile][:].rearrange("p n r -> p (n r)"),
             )
-            g_codes[tt] = codes
-            g_scales[tt] = scales
 
-        def mx_pair(acc, tt, cb, first, second):
-            for k, v in enumerate((first, second)):
+        def add_two_passes(bank, tile, cb, stationaries):
+            for k, v in enumerate(stationaries):
                 nc.tensor.matmul_mx(
-                    out=acc[:],
-                    lhsT=w_codes[cb][:, v * P : (v + 1) * P].bitcast(E4M3X4),
+                    out=bank[:],
+                    lhsT=w_words[cb][:, v * P : (v + 1) * P].bitcast(E4M3X4),
                     lhsT_scale=w_scales[cb][:, v * P : (v + 1) * P],
-                    rhs=g_codes[tt][:].bitcast(E5M2X4),
-                    rhs_scale=g_scales[tt][:],
+                    rhs=g_words[tile][:].bitcast(E5M2X4),
+                    rhs_scale=g_scales[tile][:],
                     start=(k == 0),
                     stop=(k == 1),
                 )
 
-        def butterfly(o_tile, di, s_ps, planes, r0, rows):
-            n0 = r0 * BLOCK_COLS
-            n1 = (r0 + rows) * BLOCK_COLS
+        regroup_tokens(0, 0, TILE // 2, False)
+        regroup_weights(0, HL, HH + 1)
+        regroup_weights(0, LL, LH + 1)
+        regroup_tokens(0, TILE // 2, TILE, True)
+        quantise_weights(0, HL, HH + 1)
+        negate_weights(0)
+        quantise_tokens(0)
+        quantise_weights(0, LL, LH + 1)
+        quantise_weights(0, NEG_LH, NEG_HH + 1)
+        regroup_weights(1, LL, HH + 1)
+        negate_weights(1)
+        quantise_weights(1, LL, HH + 1)
+        quantise_weights(1, NEG_LH, NEG_HH + 1)
+
+        quarters = [(tile, q) for tile in range(1, N_TILES) for q in range(4)]
+        regrouped = {}
+
+        def regroup_next_quarter():
+            if quarters:
+                tile, q = quarters.pop(0)
+                regroup_tokens(tile, q * QUARTER, (q + 1) * QUARTER, False)
+                regrouped[tile] = q + 1
+
+        for k in range(QUARTERS_AHEAD):
+            regroup_next_quarter()
+
+        to_quantise = 1
+        pixels = None
+        for h in range(HALF_UNITS):
+            tile, cb, di = h // (2 * C_BLOCKS), (h // 2) % C_BLOCKS, h % 2
+
+            t_bank = t_pool.tile([P, TILE], F32, name="t_bank")
+            add_two_passes(t_bank, tile, cb, (HL, HH if di == 0 else NEG_HH))
+            s_bank = s_pool.tile([P, TILE], F32, name="s_bank")
+            add_two_passes(s_bank, tile, cb, (LL, LH if di == 0 else NEG_LH))
+
+            planes = plane_pool.tile([P, 2, TILE], F32, name="planes")
+            nc.scalar.activation(out=planes[:, 0, :], in_=t_bank[:], func=ACT.Copy, scale=0.5)
+            regroup_next_quarter()
+            nc.gpsimd.tensor_scalar(
+                out=planes[:, 1, :], in0=planes[:, 0, :], scalar1=-1.0, scalar2=0.0, op0=ALU.mult, op1=ALU.add
+            )
+
+            if di == 0:
+                pixels = out_pool.tile([P, TILE_ROWS, 2, 2 * BLOCK_COLS], F32, name="pixels")
             nc.vector.scalar_tensor_tensor(
-                out=o_tile[:, :, di, :].rearrange("p i (j d) -> p i j d", d=2),
-                in0=s_ps[:, n0:n1].rearrange("p (i j) -> p i j", j=BLOCK_COLS).unsqueeze(3).to_broadcast([P, rows, BLOCK_COLS, 2]),
+                out=pixels[:, :, di, :].rearrange("p i (j d) -> p i j d", d=2),
+                in0=s_bank[:]
+                .rearrange("p (i j) -> p i j", j=BLOCK_COLS)
+                .unsqueeze(3)
+                .to_broadcast([P, TILE_ROWS, BLOCK_COLS, 2]),
                 scalar=0.5,
-                in1=planes[:, :, n0:n1].rearrange("p d (i j) -> p i j d", j=BLOCK_COLS),
+                in1=planes[:].rearrange("p d (i j) -> p i j d", j=BLOCK_COLS),
                 op0=ALU.mult,
                 op1=ALU.add,
             )
+            if to_quantise < N_TILES and regrouped.get(to_quantise, 0) == 4:
+                quantise_tokens(to_quantise)
+                to_quantise += 1
 
-        w_tiles(0)
-        w_tiles(1)
-        g_piece(0, 0, N_TILE // 2, False)
-        w_regroup(0, 2, 4)
-        w_regroup(0, 0, 2)
-        g_piece(0, N_TILE // 2, N_TILE, True)
-        w_quantise(0, 2, 4)
-        w_negate(0)
-        g_quantise(0)
-        w_quantise(0, 0, 2)
-        w_quantise(0, 4, 6)
-        w_regroup(1, 0, 4)
-        w_negate(1)
-        w_quantise(1, 0, 4)
-        w_quantise(1, 4, 6)
-
-        step = N_TILE // PIECES
-        pieces = [(tt, q) for tt in range(1, N_TILES) for q in range(PIECES)]
-        done = {}
-
-        def next_piece():
-            if pieces:
-                tt, q = pieces.pop(0)
-                g_piece(tt, q * step, (q + 1) * step, False)
-                done[tt] = q + 1
-
-        for k in range(EARLY_PIECES):
-            next_piece()
-
-        next_q = 1
-        halves = []
-        for h in range(4 * N_TILES):
-            tt, cb, di = h // 4, (h // 2) % 2, h % 2
-            splits = TAIL_SPLIT if h // 2 >= 2 * N_TILES - TAIL_UNITS else 1
-            rows = ROWS_TILE // splits
-            t_ps = psum_t.tile([P, N_TILE], F32, name="t_ps")
-            mx_pair(t_ps, tt, cb, HL, HH if di == 0 else NEG_HH)
-            s_ps = psum_s.tile([P, N_TILE], F32, name="s_ps")
-            mx_pair(s_ps, tt, cb, LL, LH if di == 0 else NEG_LH)
-            planes = t_pool.tile([P, 2, N_TILE], F32, name="planes")
-            nc.scalar.activation(out=planes[:, 0, :], in_=t_ps[:], func=ACT.Copy, scale=0.5)
-            next_piece()
-            nc.gpsimd.tensor_scalar(
-                out=planes[:, 1, :], in0=planes[:, 0, :], scalar1=-1.0, scalar2=0.0,
-                op0=ALU.mult, op1=ALU.add,
-            )
-            if di == 0:
-                halves = []
-            halves.append((s_ps, planes))
-            b = tt // TILES_PER_IMAGE
-            y0 = (tt % TILES_PER_IMAGE) * ROWS_TILE * 2
-            if splits == 1:
-                if di == 0:
-                    o_tile = o_pool.tile([P, rows, 2, 2 * BLOCK_COLS], F32, name="o_tile")
-                butterfly(o_tile, di, s_ps, planes, 0, rows)
-            if next_q < N_TILES and done.get(next_q, 0) == PIECES:
-                g_quantise(next_q)
-                next_q += 1
             if di == 1:
-                for r in range(splits):
-                    if splits > 1:
-                        o_tile = o_pool.tile([P, rows, 2, 2 * BLOCK_COLS], F32, name="o_tile")
-                        for dd in range(2):
-                            butterfly(o_tile, dd, halves[dd][0], halves[dd][1], r * rows, rows)
-                    ya = y0 + 2 * rows * r
-                    nc.sync.dma_start(
-                        out=out[b, cb * P : (cb + 1) * P, ya : ya + 2 * rows, :].rearrange("c y x -> c (y x)"),
-                        in_=o_tile[:].rearrange("p i d x -> p (i d x)"),
-                    )
+                image = tile // TILES_PER_IMAGE
+                row = (tile % TILES_PER_IMAGE) * 2 * TILE_ROWS
+                nc.sync.dma_start(
+                    out=out[image, cb * P : (cb + 1) * P, row : row + 2 * TILE_ROWS, :].rearrange("c y x -> c (y x)"),
+                    in_=pixels[:].rearrange("p i d x -> p (i d x)"),
+                )

@@ -36,7 +36,7 @@ N_STATIONARY = 6
 G_LOADS = ((0, 0, 1), (0, 1, 1), (0, 2, 2), (1, 0, 4))
 
 QUARTER = TILE // 4
-QUARTERS_AHEAD = 3
+QUARTERS_AHEAD = 4
 
 T_BANKS = 3
 S_BANKS = 5
@@ -163,8 +163,9 @@ def tile_haarwaveletlayer_t_kernel(tc, x, w_fusion, grad_out, out):
 
         for k in range(QUARTERS_AHEAD):
             regroup_next_quarter()
+        quantise_tokens(1)
 
-        to_quantise = 1
+        to_quantise = 2
         pixels = None
         for h in range(HALF_UNITS):
             tile, cb, di = h // (2 * C_BLOCKS), (h // 2) % C_BLOCKS, h % 2

@@ -36,10 +36,29 @@ N_STATIONARY = 6
 G_LOADS = ((0, 0, 1), (0, 1, 1), (0, 2, 2), (1, 0, 4))
 
 QUARTER = TILE // 4
-QUARTERS_AHEAD = 4
+QUARTERS_AHEAD = 1
 
+WARM_UP = 14
 T_BANKS = 3
 S_BANKS = 5
+OUT_BUFS = 6
+GROUPED_BUFS = 3
+G_QUARTERS = ()
+G_FROM = 2
+G_AHEAD = 0
+GP_SET = ()
+GP_CUTS = 2
+GP_FIRST = 1
+G_STEP = 0
+W1_ON = "V"
+W0_PIECES = 2
+G0_PIECES = 2
+G0_S = 256
+G1_WHO = "SSVV"
+G_BOTH = False
+NW0_ON = "S"
+RW1 = 1
+LAST_CUTS = 1
 
 
 def tile_haarwaveletlayer_t_kernel(tc, x, w_fusion, grad_out, out):
@@ -47,30 +66,47 @@ def tile_haarwaveletlayer_t_kernel(tc, x, w_fusion, grad_out, out):
     with ExitStack() as ctx:
         ctx.enter_context(tc.manual_schedule())
         keep = ctx.enter_context(tc.tile_pool(name="keep", bufs=1))
-        grouped_pool = ctx.enter_context(tc.tile_pool(name="grouped", bufs=3))
+        grouped_pool = ctx.enter_context(tc.tile_pool(name="grouped", bufs=GROUPED_BUFS))
         plane_pool = ctx.enter_context(tc.tile_pool(name="planes", bufs=6))
-        out_pool = ctx.enter_context(tc.tile_pool(name="outs", bufs=6))
+        out_pool = ctx.enter_context(tc.tile_pool(name="outs", bufs=OUT_BUFS))
+        half_pool = ctx.enter_context(tc.tile_pool(name="halves", bufs=2))
         t_pool = ctx.enter_context(tc.psum_pool(name="t_banks", bufs=T_BANKS))
         s_pool = ctx.enter_context(tc.psum_pool(name="s_banks", bufs=S_BANKS))
+
+        zeros = keep.tile([P, TILE], BF16, name="zeros")
+        nc.gpsimd.memset(zeros[:], 0.0)
+        for k in range(WARM_UP):
+            idle_bank = t_pool.tile([P, TILE], F32, name="t_bank")
+            nc.tensor.matmul(out=idle_bank[:], lhsT=zeros[:, 0:P], rhs=zeros[:], start=True, stop=True)
 
         w_rows = w_fusion.rearrange("(p r) k a b -> p r (k a b)", r=PACK)
         block_cols = P * BANDS
         w_raw = {}
         g_raw = {}
 
-        def load_weights(cb):
+        def load_weights(cb, pieces=1):
             w_raw[cb] = keep.tile([P, PACK, block_cols], BF16, name="w_raw%d" % cb)
-            nc.sync.dma_start(out=w_raw[cb][:], in_=w_rows[:, :, cb * block_cols : (cb + 1) * block_cols])
+            step = block_cols // pieces
+            for k in range(pieces):
+                nc.sync.dma_start(
+                    out=w_raw[cb][:, :, k * step : (k + 1) * step],
+                    in_=w_rows[:, :, cb * block_cols + k * step : cb * block_cols + (k + 1) * step],
+                )
 
-        def load_tokens(image, first, tiles):
+        def load_tokens(image, first, tiles, pieces=1):
             raw = keep.tile([P, PACK, tiles * TILE], BF16, name="g_raw%d_%d" % (image, first))
             g_rows = grad_out[image].rearrange("(p r) h w -> p r (h w)", r=PACK)
-            nc.sync.dma_start(out=raw[:], in_=g_rows[:, :, first * TILE : (first + tiles) * TILE])
+            step = tiles * TILE // pieces
+            for k in range(pieces):
+                nc.sync.dma_start(
+                    out=raw[:, :, k * step : (k + 1) * step],
+                    in_=g_rows[:, :, first * TILE + k * step : first * TILE + (k + 1) * step],
+                )
             for k in range(tiles):
                 g_raw[image * TILES_PER_IMAGE + first + k] = raw[:, :, k * TILE : (k + 1) * TILE]
 
-        load_weights(0)
-        load_tokens(*G_LOADS[0])
+        load_weights(0, W0_PIECES)
+        load_tokens(*G_LOADS[0], G0_PIECES)
         load_weights(1)
         for g_load in G_LOADS[1:]:
             load_tokens(*g_load)
@@ -83,18 +119,24 @@ def tile_haarwaveletlayer_t_kernel(tc, x, w_fusion, grad_out, out):
             w_words[cb] = keep.tile([P, N_STATIONARY * P], U32, name="w_words%d" % cb, align_bytes=64)
             w_scales[cb] = keep.tile([P, N_STATIONARY * P], U8, name="w_scales%d" % cb, align_bytes=64)
 
-        def regroup_weights(cb, first, last):
-            nc.vector.tensor_copy(
-                out=w_grouped[cb][:, first:last, :, :],
-                in_=w_raw[cb][:].rearrange("p r (c v) -> p v c r", v=BANDS)[:, first:last, :, :],
-            )
+        def regroup_weights(cb, first, last, engine="V", c0=0, c1=P):
+            dst = w_grouped[cb][:, first:last, c0:c1, :]
+            src = w_raw[cb][:].rearrange("p r (c v) -> p v c r", v=BANDS)[:, first:last, c0:c1, :]
+            if engine == "V":
+                nc.vector.tensor_copy(out=dst, in_=src)
+            elif engine == "S":
+                nc.scalar.copy(out=dst, in_=src)
+            else:
+                nc.gpsimd.tensor_scalar(out=dst, in0=src, scalar1=1.0, scalar2=0.0, op0=ALU.mult, op1=ALU.add)
 
-        def negate_weights(cb):
-            nc.vector.tensor_scalar_mul(
-                out=w_grouped[cb][:, NEG_LH : NEG_HH + 1, :, :],
-                in0=w_grouped[cb][:, LH : HH + 1 : 2, :, :],
-                scalar1=-1.0,
-            )
+        def negate_weights(cb, engine="V", c0=0, c1=P):
+            dst = w_grouped[cb][:, NEG_LH : NEG_HH + 1, c0:c1, :]
+            if engine == "V":
+                nc.vector.tensor_scalar_mul(out=dst, in0=w_grouped[cb][:, LH : HH + 1 : 2, :, :], scalar1=-1.0)
+            elif engine == "S":
+                nc.scalar.activation(out=dst, in_=w_raw[cb][:].rearrange("p r (c v) -> p v c r", v=BANDS)[:, LH : HH + 1 : 2, c0:c1, :], func=ACT.Copy, scale=-1.0)
+            else:
+                nc.gpsimd.tensor_scalar(out=dst, in0=w_raw[cb][:].rearrange("p r (c v) -> p v c r", v=BANDS)[:, LH : HH + 1 : 2, :, :], scalar1=-1.0, scalar2=0.0, op0=ALU.mult, op1=ALU.add)
 
         def quantise_weights(cb, first, last):
             nc.vector.quantize_mx(
@@ -107,15 +149,17 @@ def tile_haarwaveletlayer_t_kernel(tc, x, w_fusion, grad_out, out):
         g_words = {}
         g_scales = {}
 
-        def regroup_tokens(tile, first, last, on_vector):
+        def regroup_tokens(tile, first, last, engine):
             if tile not in g_grouped:
                 g_grouped[tile] = grouped_pool.tile([P, TILE, PACK], BF16, name="g_grouped", align_bytes=64)
             dst = g_grouped[tile][:, first:last, :].rearrange("p (c i) r -> p c r i", i=4)
             src = g_raw[tile][:, :, first:last].rearrange("p r (c i) -> p c r i", i=4)
-            if on_vector:
+            if engine == "V":
                 nc.vector.tensor_copy(out=dst, in_=src)
-            else:
+            elif engine == "S":
                 nc.scalar.copy(out=dst, in_=src)
+            else:
+                nc.gpsimd.tensor_scalar(out=dst, in0=src, scalar1=1.0, scalar2=0.0, op0=ALU.mult, op1=ALU.add)
 
         def quantise_tokens(tile):
             g_words[tile] = keep.tile([P, TILE], U32, name="g_words%d" % tile, align_bytes=64)
@@ -138,71 +182,171 @@ def tile_haarwaveletlayer_t_kernel(tc, x, w_fusion, grad_out, out):
                     stop=(k == 1),
                 )
 
-        regroup_tokens(0, 0, TILE // 2, False)
-        regroup_weights(0, HL, HH + 1)
-        regroup_weights(0, LL, LH + 1)
-        regroup_tokens(0, TILE // 2, TILE, True)
+        warm = keep.tile([P, 2], F32, name="warm")
+        nc.gpsimd.memset(warm[:, 0:1], 0.0)
+        nc.scalar.activation(out=warm[:, 1:2], in_=warm[:, 0:1], func=ACT.Copy, scale=1.0)
+        half_c = P // 2
+        if NW0_ON == "S":
+            negate_weights(0, "S", 0, half_c)
+            negate_weights(0, "S", half_c, P)
+        regroup_tokens(0, 0, G0_S, "S")
+        regroup_weights(0, LL, HH + 1, "V", 0, half_c)
+        regroup_weights(0, HL, HH + 1, "V", half_c, P)
+        regroup_weights(0, LL, LH + 1, "V", half_c, P)
         quantise_weights(0, HL, HH + 1)
-        negate_weights(0)
-        quantise_tokens(0)
         quantise_weights(0, LL, LH + 1)
-        quantise_weights(0, NEG_LH, NEG_HH + 1)
-        regroup_weights(1, LL, HH + 1)
-        negate_weights(1)
-        quantise_weights(1, LL, HH + 1)
+        regroup_tokens(0, G0_S, TILE, "V")
+        if NW0_ON == "S":
+            quantise_weights(0, NEG_LH, NEG_HH + 1)
+        if NW0_ON == "V":
+            negate_weights(0, "V")
+        quantise_tokens(0)
+        if RW1 == 0:
+            negate_weights(1, "S")
+            regroup_weights(1, LL, HH + 1, "V")
+            quantise_weights(0, NEG_LH, NEG_HH + 1)
+        elif RW1 == 1:
+            regroup_weights(1, HL, HH + 1, "S")
+            regroup_weights(1, LL, LH + 1, "V")
+            quantise_weights(1, HL, HH + 1)
+            negate_weights(1, "V")
+        else:
+            regroup_weights(1, LL, HH + 1, "V")
+            quantise_weights(0, NEG_LH, NEG_HH + 1)
+            negate_weights(1, "V")
+        quantise_weights(1, LL, LH + 1)
         quantise_weights(1, NEG_LH, NEG_HH + 1)
 
-        quarters = [(tile, q) for tile in range(1, N_TILES) for q in range(4)]
+        def who(tile, q):
+            if tile == 1:
+                return G1_WHO[q]
+            return "G" if (tile >= G_FROM and q in G_QUARTERS) else "S"
+
+        s_jobs = [(tile, q) for tile in range(1, N_TILES) for q in range(4) if who(tile, q) == "S"]
+        g_jobs = [(tile, q) for tile in range(1, N_TILES) for q in range(4) if who(tile, q) == "G"]
+        v_jobs = [(tile, q) for tile in range(1, N_TILES) for q in range(4) if who(tile, q) == "V"]
         regrouped = {}
 
-        def regroup_next_quarter():
-            if quarters:
-                tile, q = quarters.pop(0)
-                regroup_tokens(tile, q * QUARTER, (q + 1) * QUARTER, False)
-                regrouped[tile] = q + 1
+        def regroup_next(jobs, engine):
+            if jobs:
+                tile, q = jobs.pop(0)
+                regroup_tokens(tile, q * QUARTER, (q + 1) * QUARTER, engine)
+                regrouped[tile] = regrouped.get(tile, 0) + 1
 
         for k in range(QUARTERS_AHEAD):
-            regroup_next_quarter()
-        quantise_tokens(1)
+            regroup_next(s_jobs, "S")
+        for k in range(G_AHEAD):
+            regroup_next(g_jobs, "G")
+        while v_jobs:
+            regroup_next(v_jobs, "V")
+        state = {"to_quantise": 1}
 
-        to_quantise = 2
-        pixels = None
+        pixel_tiles = {}
+        waiting = []
+        left = {}
+
+        def store(unit, rows):
+            tile, cb = unit // C_BLOCKS, unit % C_BLOCKS
+            image = tile // TILES_PER_IMAGE
+            row = (tile % TILES_PER_IMAGE) * 2 * TILE_ROWS
+            nc.sync.dma_start(
+                out=out[image, cb * P : (cb + 1) * P, row + 2 * rows.start : row + 2 * rows.stop, :].rearrange("c y x -> c (y x)"),
+                in_=pixel_tiles[unit][:, rows, :, :].rearrange("p i d x -> p (i d x)"),
+            )
+
+        def wrote(unit, rows):
+            key = (unit, rows.start)
+            left[key] -= 1
+            if left[key] == 0:
+                store(unit, rows)
+
+        def issue_piece():
+            if waiting:
+                unit, di, s_half, t_half, rows, op, group = waiting.pop(0)
+                dj = 0 if op == ALU.add else 1
+                nc.gpsimd.tensor_tensor(
+                    out=pixel_tiles[unit][:, rows, di, :].rearrange("p i (j d) -> p i j d", d=2)[:, :, :, dj],
+                    in0=s_half[:].rearrange("p (i j) -> p i j", j=BLOCK_COLS)[:, rows, :],
+                    in1=t_half[:].rearrange("p (i j) -> p i j", j=BLOCK_COLS)[:, rows, :],
+                    op=op,
+                )
+                wrote(unit, group)
+                return True
+            return False
+
+        def g_extras(h):
+            if h % 4 == G_STEP and g_jobs:
+                regroup_next(g_jobs, "G")
+                if G_BOTH:
+                    issue_piece()
+            else:
+                issue_piece()
+
+        def maybe_quantise():
+            tq = state["to_quantise"]
+            if tq < N_TILES and regrouped.get(tq, 0) == 4:
+                quantise_tokens(tq)
+                state["to_quantise"] = tq + 1
+
         for h in range(HALF_UNITS):
             tile, cb, di = h // (2 * C_BLOCKS), (h // 2) % C_BLOCKS, h % 2
+            unit = h // 2
+            on_gpsimd = h in GP_SET
+            cuts = LAST_CUTS if unit == HALF_UNITS // 2 - 1 else 1
+            groups = [slice(k * TILE_ROWS // cuts, (k + 1) * TILE_ROWS // cuts) for k in range(cuts)]
 
             t_bank = t_pool.tile([P, TILE], F32, name="t_bank")
             add_two_passes(t_bank, tile, cb, (HL, HH if di == 0 else NEG_HH))
             s_bank = s_pool.tile([P, TILE], F32, name="s_bank")
             add_two_passes(s_bank, tile, cb, (LL, LH if di == 0 else NEG_LH))
 
-            planes = plane_pool.tile([P, 2, TILE], F32, name="planes")
-            nc.scalar.activation(out=planes[:, 0, :], in_=t_bank[:], func=ACT.Copy, scale=0.5)
-            regroup_next_quarter()
-            nc.gpsimd.tensor_scalar(
-                out=planes[:, 1, :], in0=planes[:, 0, :], scalar1=-1.0, scalar2=0.0, op0=ALU.mult, op1=ALU.add
-            )
-
             if di == 0:
-                pixels = out_pool.tile([P, TILE_ROWS, 2, 2 * BLOCK_COLS], F32, name="pixels")
-            nc.vector.scalar_tensor_tensor(
-                out=pixels[:, :, di, :].rearrange("p i (j d) -> p i j d", d=2),
-                in0=s_bank[:]
-                .rearrange("p (i j) -> p i j", j=BLOCK_COLS)
-                .unsqueeze(3)
-                .to_broadcast([P, TILE_ROWS, BLOCK_COLS, 2]),
-                scalar=0.5,
-                in1=planes[:].rearrange("p d (i j) -> p i j d", j=BLOCK_COLS),
-                op0=ALU.mult,
-                op1=ALU.add,
-            )
-            if to_quantise < N_TILES and regrouped.get(to_quantise, 0) == 4:
-                quantise_tokens(to_quantise)
-                to_quantise += 1
+                pixel_tiles[unit] = out_pool.tile([P, TILE_ROWS, 2, 2 * BLOCK_COLS], F32, name="pixels")
+                for grp in groups:
+                    left[(unit, grp.start)] = sum(2 * GP_CUTS if k in GP_SET else 1 for k in (h, h + 1))
 
-            if di == 1:
-                image = tile // TILES_PER_IMAGE
-                row = (tile % TILES_PER_IMAGE) * 2 * TILE_ROWS
-                nc.sync.dma_start(
-                    out=out[image, cb * P : (cb + 1) * P, row : row + 2 * TILE_ROWS, :].rearrange("c y x -> c (y x)"),
-                    in_=pixels[:].rearrange("p i d x -> p (i d x)"),
+            if on_gpsimd:
+                t_half = half_pool.tile([P, TILE], F32, name="t_half")
+                nc.scalar.activation(out=t_half[:], in_=t_bank[:], func=ACT.Copy, scale=0.5)
+                s_half = half_pool.tile([P, TILE], F32, name="s_half")
+                nc.scalar.activation(out=s_half[:], in_=s_bank[:], func=ACT.Copy, scale=0.5)
+                regroup_next(s_jobs, "S")
+                step = TILE_ROWS // GP_CUTS
+                for k in range(GP_CUTS):
+                    for op in (ALU.add, ALU.subtract):
+                        waiting.append((unit, di, s_half, t_half, slice(k * step, (k + 1) * step), op, groups[0]))
+                if h % 4 == G_STEP and g_jobs:
+                    regroup_next(g_jobs, "G")
+                for k in range(GP_FIRST):
+                    issue_piece()
+            else:
+                planes = plane_pool.tile([P, 2, TILE], F32, name="planes")
+                nc.scalar.activation(out=planes[:, 0, :], in_=t_bank[:], func=ACT.Copy, scale=0.5)
+                regroup_next(s_jobs, "S")
+                nc.gpsimd.tensor_scalar(
+                    out=planes[:, 1, :], in0=planes[:, 0, :], scalar1=-1.0, scalar2=0.0, op0=ALU.mult, op1=ALU.add
                 )
+                g_extras(h)
+                if cuts == 1 or di == 0:
+                    todo = [(di, grp) for grp in groups] if cuts == 1 else []
+                else:
+                    todo = [(d, grp) for grp in groups for d in (0, 1)]
+                if cuts > 1 and di == 0:
+                    held = (s_bank, planes)
+                for d, grp in todo:
+                    sb, pl = (s_bank, planes) if d == di else held
+                    nc.vector.scalar_tensor_tensor(
+                        out=pixel_tiles[unit][:, grp, d, :].rearrange("p i (j d) -> p i j d", d=2),
+                        in0=sb[:]
+                        .rearrange("p (i j) -> p i j", j=BLOCK_COLS)[:, grp, :]
+                        .unsqueeze(3)
+                        .to_broadcast([P, grp.stop - grp.start, BLOCK_COLS, 2]),
+                        scalar=0.5,
+                        in1=pl[:].rearrange("p d (i j) -> p i j d", j=BLOCK_COLS)[:, grp, :, :],
+                        op0=ALU.mult,
+                        op1=ALU.add,
+                    )
+                    wrote(unit, grp)
+            maybe_quantise()
+        while waiting:
+            issue_piece()

@@ -36,9 +36,9 @@ N_STATIONARY = 6
 G_LOADS = ((0, 0, 1), (0, 1, 1), (0, 2, 2), (1, 0, 4))
 
 QUARTER = TILE // 4
-QUARTERS_AHEAD = 1
+QUARTERS_AHEAD = 0
 
-WARM_UP = 14
+WARM_UP = 12
 T_BANKS = 3
 S_BANKS = 5
 OUT_BUFS = 6
@@ -186,34 +186,22 @@ def tile_haarwaveletlayer_t_kernel(tc, x, w_fusion, grad_out, out):
         nc.gpsimd.memset(warm[:, 0:1], 0.0)
         nc.scalar.activation(out=warm[:, 1:2], in_=warm[:, 0:1], func=ACT.Copy, scale=1.0)
         half_c = P // 2
-        if NW0_ON == "S":
-            negate_weights(0, "S", 0, half_c)
-            negate_weights(0, "S", half_c, P)
         regroup_tokens(0, 0, G0_S, "S")
+        negate_weights(0, "S", 0, P)
+        regroup_weights(1, HL, HH + 1, "S")
         regroup_weights(0, LL, HH + 1, "V", 0, half_c)
         regroup_weights(0, HL, HH + 1, "V", half_c, P)
         regroup_weights(0, LL, LH + 1, "V", half_c, P)
         quantise_weights(0, HL, HH + 1)
-        quantise_weights(0, LL, LH + 1)
         regroup_tokens(0, G0_S, TILE, "V")
-        if NW0_ON == "S":
-            quantise_weights(0, NEG_LH, NEG_HH + 1)
-        if NW0_ON == "V":
-            negate_weights(0, "V")
+        quantise_weights(0, LL, LH + 1)
         quantise_tokens(0)
-        if RW1 == 0:
-            negate_weights(1, "S")
-            regroup_weights(1, LL, HH + 1, "V")
-            quantise_weights(0, NEG_LH, NEG_HH + 1)
-        elif RW1 == 1:
-            regroup_weights(1, HL, HH + 1, "S")
-            regroup_weights(1, LL, LH + 1, "V")
-            quantise_weights(1, HL, HH + 1)
-            negate_weights(1, "V")
-        else:
-            regroup_weights(1, LL, HH + 1, "V")
-            quantise_weights(0, NEG_LH, NEG_HH + 1)
-            negate_weights(1, "V")
+        regroup_weights(1, LL, LH + 1, "V")
+        quantise_weights(0, NEG_LH, NEG_HH + 1)
+        regroup_tokens(1, 2 * QUARTER, 3 * QUARTER, "V")
+        regroup_tokens(1, 3 * QUARTER, TILE, "V")
+        quantise_weights(1, HL, HH + 1)
+        negate_weights(1, "V")
         quantise_weights(1, LL, LH + 1)
         quantise_weights(1, NEG_LH, NEG_HH + 1)
 
@@ -237,8 +225,7 @@ def tile_haarwaveletlayer_t_kernel(tc, x, w_fusion, grad_out, out):
             regroup_next(s_jobs, "S")
         for k in range(G_AHEAD):
             regroup_next(g_jobs, "G")
-        while v_jobs:
-            regroup_next(v_jobs, "V")
+        regrouped[1] = len(v_jobs)
         state = {"to_quantise": 1}
 
         pixel_tiles = {}
@@ -323,6 +310,8 @@ def tile_haarwaveletlayer_t_kernel(tc, x, w_fusion, grad_out, out):
                 planes = plane_pool.tile([P, 2, TILE], F32, name="planes")
                 nc.scalar.activation(out=planes[:, 0, :], in_=t_bank[:], func=ACT.Copy, scale=0.5)
                 regroup_next(s_jobs, "S")
+                if h == 0:
+                    regroup_next(s_jobs, "S")
                 nc.gpsimd.tensor_scalar(
                     out=planes[:, 1, :], in0=planes[:, 0, :], scalar1=-1.0, scalar2=0.0, op0=ALU.mult, op1=ALU.add
                 )

@@ -38,7 +38,10 @@ G_LOADS = ((0, 0, 1), (0, 1, 1), (0, 2, 2), (1, 0, 4))
 QUARTER = TILE // 4
 QUARTERS_AHEAD = 0
 
-WARM_UP = 12
+WARM_UP = 8
+WARM_W = 4
+WARM_G = 4
+S_FIRST = 2
 T_BANKS = 3
 S_BANKS = 5
 OUT_BUFS = 6
@@ -111,6 +114,13 @@ def tile_haarwaveletlayer_t_kernel(tc, x, w_fusion, grad_out, out):
         for g_load in G_LOADS[1:]:
             load_tokens(*g_load)
 
+        for k in range(WARM_W):
+            idle_bank = t_pool.tile([P, TILE], F32, name="t_bank")
+            nc.tensor.matmul(out=idle_bank[:], lhsT=w_raw[0][:, 0, 0:P], rhs=w_raw[0][:, 1, :], start=True, stop=True)
+        for k in range(WARM_G):
+            idle_bank = t_pool.tile([P, TILE], F32, name="t_bank")
+            nc.tensor.matmul(out=idle_bank[:], lhsT=w_raw[0][:, 0, 0:P], rhs=g_raw[0][:, 0, :], start=True, stop=True)
+
         w_grouped = {}
         w_words = {}
         w_scales = {}
@@ -137,6 +147,14 @@ def tile_haarwaveletlayer_t_kernel(tc, x, w_fusion, grad_out, out):
                 nc.scalar.activation(out=dst, in_=w_raw[cb][:].rearrange("p r (c v) -> p v c r", v=BANDS)[:, LH : HH + 1 : 2, c0:c1, :], func=ACT.Copy, scale=-1.0)
             else:
                 nc.gpsimd.tensor_scalar(out=dst, in0=w_raw[cb][:].rearrange("p r (c v) -> p v c r", v=BANDS)[:, LH : HH + 1 : 2, :, :], scalar1=-1.0, scalar2=0.0, op0=ALU.mult, op1=ALU.add)
+
+        def negate_band(cb, band, slot):
+            nc.scalar.activation(
+                out=w_grouped[cb][:, slot, :, :],
+                in_=w_raw[cb][:].rearrange("p r (c v) -> p v c r", v=BANDS)[:, band, :, :],
+                func=ACT.Copy,
+                scale=-1.0,
+            )
 
         def quantise_weights(cb, first, last):
             nc.vector.quantize_mx(
@@ -186,8 +204,9 @@ def tile_haarwaveletlayer_t_kernel(tc, x, w_fusion, grad_out, out):
         nc.gpsimd.memset(warm[:, 0:1], 0.0)
         nc.scalar.activation(out=warm[:, 1:2], in_=warm[:, 0:1], func=ACT.Copy, scale=1.0)
         half_c = P // 2
+        negate_band(0, LH, NEG_LH)
         regroup_tokens(0, 0, G0_S, "S")
-        negate_weights(0, "S", 0, P)
+        negate_band(0, HH, NEG_HH)
         regroup_weights(1, HL, HH + 1, "S")
         regroup_weights(0, LL, HH + 1, "V", 0, half_c)
         regroup_weights(0, HL, HH + 1, "V", half_c, P)
@@ -198,7 +217,8 @@ def tile_haarwaveletlayer_t_kernel(tc, x, w_fusion, grad_out, out):
         quantise_tokens(0)
         regroup_weights(1, LL, LH + 1, "V")
         quantise_weights(0, NEG_LH, NEG_HH + 1)
-        regroup_tokens(1, 2 * QUARTER, 3 * QUARTER, "V")
+        if G1_WHO[2] == "V":
+            regroup_tokens(1, 2 * QUARTER, 3 * QUARTER, "V")
         regroup_tokens(1, 3 * QUARTER, TILE, "V")
         quantise_weights(1, HL, HH + 1)
         negate_weights(1, "V")
@@ -311,7 +331,8 @@ def tile_haarwaveletlayer_t_kernel(tc, x, w_fusion, grad_out, out):
                 nc.scalar.activation(out=planes[:, 0, :], in_=t_bank[:], func=ACT.Copy, scale=0.5)
                 regroup_next(s_jobs, "S")
                 if h == 0:
-                    regroup_next(s_jobs, "S")
+                    for k in range(S_FIRST - 1):
+                        regroup_next(s_jobs, "S")
                 nc.gpsimd.tensor_scalar(
                     out=planes[:, 1, :], in0=planes[:, 0, :], scalar1=-1.0, scalar2=0.0, op0=ALU.mult, op1=ALU.add
                 )

from contextlib import ExitStack

import concourse.mybir as mybir

F32 = mybir.dt.float32
BF16 = mybir.dt.bfloat16
U32 = mybir.dt.uint32
U8 = mybir.dt.uint8
E4M3X4 = mybir.dt.float8_e4m3fn_x4
E5M2X4 = mybir.dt.float8_e5m2_x4
ALU = mybir.AluOpType
ACT = mybir.ActivationFunctionType

P = 128
PACK = 4
IMAGES = 2
CHANNELS = 256
OUT_CH = 512
BANDS = 4
BLOCK_ROWS = 64
BLOCK_COLS = 32
TOKENS = BLOCK_ROWS * BLOCK_COLS
TILE = 512
TILE_ROWS = TILE // BLOCK_COLS
TILES_PER_IMAGE = TOKENS // TILE
N_TILES = IMAGES * TILES_PER_IMAGE
C_BLOCKS = CHANNELS // P
HALF_UNITS = N_TILES * C_BLOCKS * 2

FLOPS = 2 * IMAGES * TOKENS * OUT_CH * CHANNELS * BANDS
BYTES = 2 * OUT_CH * CHANNELS * BANDS + 2 * IMAGES * OUT_CH * TOKENS + 4 * IMAGES * CHANNELS * 4 * TOKENS

LL, LH, HL, HH, NEG_LH, NEG_HH = 0, 1, 2, 3, 4, 5
N_STATIONARY = 6

G_LOADS = ((0, 0, 1), (0, 1, 1), (0, 2, 2), (1, 0, 4))

QUARTER = TILE // 4
QUARTERS_AHEAD = 0

WARM_UP = 8
WARM_W = 4
WARM_G = 4
S_FIRST = 2
T_BANKS = 3
S_BANKS = 5
OUT_BUFS = 6
GROUPED_BUFS = 3
G_QUARTERS = ()
G_FROM = 2
G_AHEAD = 0
GP_SET = ()
GP_CUTS = 2
GP_FIRST = 1
G_STEP = 0
W1_ON = "V"
W0_PIECES = 2
G0_PIECES = 2
G0_S = 256
G1_WHO = "SSVV"
G_BOTH = False
NW0_ON = "S"
RW1 = 1
LAST_CUTS = 1


def tile_haarwaveletlayer_t_kernel(tc, x, w_fusion, grad_out, out):
    nc = tc.nc
    with ExitStack() as ctx:
        ctx.enter_context(tc.manual_schedule())
        keep = ctx.enter_context(tc.tile_pool(name="keep", bufs=1))
        grouped_pool = ctx.enter_context(tc.tile_pool(name="grouped", bufs=GROUPED_BUFS))
        plane_pool = ctx.enter_context(tc.tile_pool(name="planes", bufs=6))
        out_pool = ctx.enter_context(tc.tile_pool(name="outs", bufs=OUT_BUFS))
        half_pool = ctx.enter_context(tc.tile_pool(name="halves", bufs=2))
        t_pool = ctx.enter_context(tc.psum_pool(name="t_banks", bufs=T_BANKS))
        s_pool = ctx.enter_context(tc.psum_pool(name="s_banks", bufs=S_BANKS))

        zeros = keep.tile([P, TILE], BF16, name="zeros")
        nc.gpsimd.memset(zeros[:], 0.0)
        for k in range(WARM_UP):
            idle_bank = t_pool.tile([P, TILE], F32, name="t_bank")
            nc.tensor.matmul(out=idle_bank[:], lhsT=zeros[:, 0:P], rhs=zeros[:], start=True, stop=True)

        w_rows = w_fusion.rearrange("(p r) k a b -> p r (k a b)", r=PACK)
        block_cols = P * BANDS
        w_raw = {}
        g_raw = {}

        def load_weights(cb, pieces=1):
            w_raw[cb] = keep.tile([P, PACK, block_cols], BF16, name="w_raw%d" % cb)
            step = block_cols // pieces
            for k in range(pieces):
                nc.sync.dma_start(
                    out=w_raw[cb][:, :, k * step : (k + 1) * step],
                    in_=w_rows[:, :, cb * block_cols + k * step : cb * block_cols + (k + 1) * step],
                )

        def load_tokens(image, first, tiles, pieces=1):
            raw = keep.tile([P, PACK, tiles * TILE], BF16, name="g_raw%d_%d" % (image, first))
            g_rows = grad_out[image].rearrange("(p r) h w -> p r (h w)", r=PACK)
            step = tiles * TILE // pieces
            for k in range(pieces):
                nc.sync.dma_start(
                    out=raw[:, :, k * step : (k + 1) * step],
                    in_=g_rows[:, :, first * TILE + k * step : first * TILE + (k + 1) * step],
                )
            for k in range(tiles):
                g_raw[image * TILES_PER_IMAGE + first + k] = raw[:, :, k * TILE : (k + 1) * TILE]

        load_weights(0, W0_PIECES)
        load_tokens(*G_LOADS[0], G0_PIECES)
        load_weights(1)
        for g_load in G_LOADS[1:]:
            load_tokens(*g_load)

        for k in range(WARM_W):
            idle_bank = t_pool.tile([P, TILE], F32, name="t_bank")
            nc.tensor.matmul(out=idle_bank[:], lhsT=w_raw[0][:, 0, 0:P], rhs=w_raw[0][:, 1, :], start=True, stop=True)
        for k in range(WARM_G):
            idle_bank = t_pool.tile([P, TILE], F32, name="t_bank")
            nc.tensor.matmul(out=idle_bank[:], lhsT=w_raw[0][:, 0, 0:P], rhs=g_raw[0][:, 0, :], start=True, stop=True)

        w_grouped = {}
        w_words = {}
        w_scales = {}
        for cb in range(C_BLOCKS):
            w_grouped[cb] = keep.tile([P, N_STATIONARY, P, PACK], BF16, name="w_grouped%d" % cb, align_bytes=64)
            w_words[cb] = keep.tile([P, N_STATIONARY * P], U32, name="w_words%d" % cb, align_bytes=64)
            w_scales[cb] = keep.tile([P, N_STATIONARY * P], U8, name="w_scales%d" % cb, align_bytes=64)

        def regroup_weights(cb, first, last, engine="V", c0=0, c1=P):
            dst = w_grouped[cb][:, first:last, c0:c1, :]
            src = w_raw[cb][:].rearrange("p r (c v) -> p v c r", v=BANDS)[:, first:last, c0:c1, :]
            if engine == "V":
                nc.vector.tensor_copy(out=dst, in_=src)
            elif engine == "S":
                nc.scalar.copy(out=dst, in_=src)
            else:
                nc.gpsimd.tensor_scalar(out=dst, in0=src, scalar1=1.0, scalar2=0.0, op0=ALU.mult, op1=ALU.add)

        def negate_weights(cb, engine="V", c0=0, c1=P):
            dst = w_grouped[cb][:, NEG_LH : NEG_HH + 1, c0:c1, :]
            if engine == "V":
                nc.vector.tensor_scalar_mul(out=dst, in0=w_grouped[cb][:, LH : HH + 1 : 2, :, :], scalar1=-1.0)
            elif engine == "S":
                nc.scalar.activation(out=dst, in_=w_raw[cb][:].rearrange("p r (c v) -> p v c r", v=BANDS)[:, LH : HH + 1 : 2, c0:c1, :], func=ACT.Copy, scale=-1.0)
            else:
                nc.gpsimd.tensor_scalar(out=dst, in0=w_raw[cb][:].rearrange("p r (c v) -> p v c r", v=BANDS)[:, LH : HH + 1 : 2, :, :], scalar1=-1.0, scalar2=0.0, op0=ALU.mult, op1=ALU.add)

        def negate_band(cb, band, slot):
            nc.scalar.activation(
                out=w_grouped[cb][:, slot, :, :],
                in_=w_raw[cb][:].rearrange("p r (c v) -> p v c r", v=BANDS)[:, band, :, :],
                func=ACT.Copy,
                scale=-1.0,
            )

        def quantise_weights(cb, first, last):
            nc.vector.quantize_mx(
                out=w_words[cb][:, first * P : last * P].bitcast(E4M3X4),
                scales=w_scales[cb][:, first * P : last * P],
                in_=w_grouped[cb][:, first:last, :, :].rearrange("p v c r -> p (v c r)"),
            )

        g_grouped = {}
        g_words = {}
        g_scales = {}

        def regroup_tokens(tile, first, last, engine):
            if tile not in g_grouped:
                g_grouped[tile] = grouped_pool.tile([P, TILE, PACK], BF16, name="g_grouped", align_bytes=64)
            dst = g_grouped[tile][:, first:last, :].rearrange("p (c i) r -> p c r i", i=4)
            src = g_raw[tile][:, :, first:last].rearrange("p r (c i) -> p c r i", i=4)
            if engine == "V":
                nc.vector.tensor_copy(out=dst, in_=src)
            elif engine == "S":
                nc.scalar.copy(out=dst, in_=src)
            else:
                nc.gpsimd.tensor_scalar(out=dst, in0=src, scalar1=1.0, scalar2=0.0, op0=ALU.mult, op1=ALU.add)

        def quantise_tokens(tile):
            g_words[tile] = keep.tile([P, TILE], U32, name="g_words%d" % tile, align_bytes=64)
            g_scales[tile] = keep.tile([P, TILE], U8, name="g_scales%d" % tile, align_bytes=64)
            nc.vector.quantize_mx(
                out=g_words[tile][:].bitcast(E5M2X4),
                scales=g_scales[tile][:],
                in_=g_grouped[tile][:].rearrange("p n r -> p (n r)"),
            )

        def add_two_passes(bank, tile, cb, stationaries):
            for k, v in enumerate(stationaries):
                nc.tensor.matmul_mx(
                    out=bank[:],
                    lhsT=w_words[cb][:, v * P : (v + 1) * P].bitcast(E4M3X4),
                    lhsT_scale=w_scales[cb][:, v * P : (v + 1) * P],
                    rhs=g_words[tile][:].bitcast(E5M2X4),
                    rhs_scale=g_scales[tile][:],
                    start=(k == 0),
                    stop=(k == 1),
                )

        warm = keep.tile([P, 2], F32, name="warm")
        nc.gpsimd.memset(warm[:, 0:1], 0.0)
        nc.scalar.activation(out=warm[:, 1:2], in_=warm[:, 0:1], func=ACT.Copy, scale=1.0)
        half_c = P // 2
        negate_band(0, LH, NEG_LH)
        regroup_tokens(0, 0, G0_S, "S")
        negate_band(0, HH, NEG_HH)
        regroup_weights(1, HL, HH + 1, "S")
        regroup_weights(0, LL, HH + 1, "V", 0, half_c)
        regroup_weights(0, HL, HH + 1, "V", half_c, P)
        regroup_weights(0, LL, LH + 1, "V", half_c, P)
        quantise_weights(0, HL, HH + 1)
        regroup_tokens(0, G0_S, TILE, "V")
        quantise_weights(0, LL, LH + 1)
        quantise_tokens(0)
        regroup_weights(1, LL, LH + 1, "V")
        quantise_weights(0, NEG_LH, NEG_HH + 1)
        if G1_WHO[2] == "V":
            regroup_tokens(1, 2 * QUARTER, 3 * QUARTER, "V")
        regroup_tokens(1, 3 * QUARTER, TILE, "V")
        quantise_weights(1, HL, HH + 1)
        negate_weights(1, "V")
        quantise_weights(1, LL, LH + 1)
        quantise_weights(1, NEG_LH, NEG_HH + 1)

        def who(tile, q):
            if tile == 1:
                return G1_WHO[q]
            return "G" if (tile >= G_FROM and q in G_QUARTERS) else "S"

        s_jobs = [(tile, q) for tile in range(1, N_TILES) for q in range(4) if who(tile, q) == "S"]
        g_jobs = [(tile, q) for tile in range(1, N_TILES) for q in range(4) if who(tile, q) == "G"]
        v_jobs = [(tile, q) for tile in range(1, N_TILES) for q in range(4) if who(tile, q) == "V"]
        regrouped = {}

        def regroup_next(jobs, engine):
            if jobs:
                tile, q = jobs.pop(0)
                regroup_tokens(tile, q * QUARTER, (q + 1) * QUARTER, engine)
                regrouped[tile] = regrouped.get(tile, 0) + 1

        for k in range(QUARTERS_AHEAD):
            regroup_next(s_jobs, "S")
        for k in range(G_AHEAD):
            regroup_next(g_jobs, "G")
        regrouped[1] = len(v_jobs)
        state = {"to_quantise": 1}

        pixel_tiles = {}
        waiting = []
        left = {}

        def store(unit, rows):
            tile, cb = unit // C_BLOCKS, unit % C_BLOCKS
            image = tile // TILES_PER_IMAGE
            row = (tile % TILES_PER_IMAGE) * 2 * TILE_ROWS
            nc.sync.dma_start(
                out=out[image, cb * P : (cb + 1) * P, row + 2 * rows.start : row + 2 * rows.stop, :].rearrange("c y x -> c (y x)"),
                in_=pixel_tiles[unit][:, rows, :, :].rearrange("p i d x -> p (i d x)"),
            )

        def wrote(unit, rows):
            key = (unit, rows.start)
            left[key] -= 1
            if left[key] == 0:
                store(unit, rows)

        def issue_piece():
            if waiting:
                unit, di, s_half, t_half, rows, op, group = waiting.pop(0)
                dj = 0 if op == ALU.add else 1
                nc.gpsimd.tensor_tensor(
                    out=pixel_tiles[unit][:, rows, di, :].rearrange("p i (j d) -> p i j d", d=2)[:, :, :, dj],
                    in0=s_half[:].rearrange("p (i j) -> p i j", j=BLOCK_COLS)[:, rows, :],
                    in1=t_half[:].rearrange("p (i j) -> p i j", j=BLOCK_COLS)[:, rows, :],
                    op=op,
                )
                wrote(unit, group)
                return True
            return False

        def g_extras(h):
            if h % 4 == G_STEP and g_jobs:
                regroup_next(g_jobs, "G")
                if G_BOTH:
                    issue_piece()
            else:
                issue_piece()

        def maybe_quantise():
            tq = state["to_quantise"]
            if tq < N_TILES and regrouped.get(tq, 0) == 4:
                quantise_tokens(tq)
                state["to_quantise"] = tq + 1

        for h in range(HALF_UNITS):
            tile, cb, di = h // (2 * C_BLOCKS), (h // 2) % C_BLOCKS, h % 2
            unit = h // 2
            on_gpsimd = h in GP_SET
            cuts = LAST_CUTS if unit == HALF_UNITS // 2 - 1 else 1
            groups = [slice(k * TILE_ROWS // cuts, (k + 1) * TILE_ROWS // cuts) for k in range(cuts)]

            t_bank = t_pool.tile([P, TILE], F32, name="t_bank")
            add_two_passes(t_bank, tile, cb, (HL, HH if di == 0 else NEG_HH))
            s_bank = s_pool.tile([P, TILE], F32, name="s_bank")
            add_two_passes(s_bank, tile, cb, (LL, LH if di == 0 else NEG_LH))

            if di == 0:
                pixel_tiles[unit] = out_pool.tile([P, TILE_ROWS, 2, 2 * BLOCK_COLS], F32, name="pixels")
                for grp in groups:
                    left[(unit, grp.start)] = sum(2 * GP_CUTS if k in GP_SET else 1 for k in (h, h + 1))

            if on_gpsimd:
                t_half = half_pool.tile([P, TILE], F32, name="t_half")
                nc.scalar.activation(out=t_half[:], in_=t_bank[:], func=ACT.Copy, scale=0.5)
                s_half = half_pool.tile([P, TILE], F32, name="s_half")
                nc.scalar.activation(out=s_half[:], in_=s_bank[:], func=ACT.Copy, scale=0.5)
                regroup_next(s_jobs, "S")
                step = TILE_ROWS // GP_CUTS
                for k in range(GP_CUTS):
                    for op in (ALU.add, ALU.subtract):
                        waiting.append((unit, di, s_half, t_half, slice(k * step, (k + 1) * step), op, groups[0]))
                if h % 4 == G_STEP and g_jobs:
                    regroup_next(g_jobs, "G")
                for k in range(GP_FIRST):
                    issue_piece()
            else:
                planes = plane_pool.tile([P, 2, TILE], F32, name="planes")
                nc.scalar.activation(out=planes[:, 0, :], in_=t_bank[:], func=ACT.Copy, scale=0.5)
                regroup_next(s_jobs, "S")
                if h == 0:
                    for k in range(S_FIRST - 1):
                        regroup_next(s_jobs, "S")
                nc.gpsimd.tensor_scalar(
                    out=planes[:, 1, :], in0=planes[:, 0, :], scalar1=-1.0, scalar2=0.0, op0=ALU.mult, op1=ALU.add
                )
                g_extras(h)
                if cuts == 1 or di == 0:
                    todo = [(di, grp) for grp in groups] if cuts == 1 else []
                else:
                    todo = [(d, grp) for grp in groups for d in (0, 1)]
                if cuts > 1 and di == 0:
                    held = (s_bank, planes)
                for d, grp in todo:
                    sb, pl = (s_bank, planes) if d == di else held
                    nc.vector.scalar_tensor_tensor(
                        out=pixel_tiles[unit][:, grp, d, :].rearrange("p i (j d) -> p i j d", d=2),
                        in0=sb[:]
                        .rearrange("p (i j) -> p i j", j=BLOCK_COLS)[:, grp, :]
                        .unsqueeze(3)
                        .to_broadcast([P, grp.stop - grp.start, BLOCK_COLS, 2]),
                        scalar=0.5,
                        in1=pl[:].rearrange("p d (i j) -> p i j d", j=BLOCK_COLS)[:, grp, :, :],
                        op0=ALU.mult,
                        op1=ALU.add,
                    )
                    wrote(unit, grp)
            maybe_quantise()
        while waiting:
            issue_piece()
